import numpy as np
import ml_dtypes


def mxq(x, axis, fmt="e4m3"):
    dtype, down = {"e4m3": (ml_dtypes.float8_e4m3fn, 7), "e5m2": (ml_dtypes.float8_e5m2, 14)}[fmt]
    v = np.moveaxis(np.asarray(x, np.float32).astype(ml_dtypes.bfloat16).astype(np.float64), axis, -1)
    blocks = v.reshape(v.shape[:-1] + (-1, 32))
    amax = np.abs(blocks).max(-1, keepdims=True)
    byte = np.maximum(np.where(amax > 0, np.frexp(amax)[1] - 1 + 127, 0) - down, 1)
    scale = np.exp2(byte - 127.0)
    codes = (blocks / scale).astype(np.float32).astype(dtype).astype(np.float64)
    return np.moveaxis((codes * scale).reshape(v.shape), -1, axis)


WIDE = False


def mx_kscale(k):
    if not WIDE:
        return np.ones(k)
    levels = np.array([10, -10, 5, -5, 0])
    if k % 512:
        return np.exp2(np.random.permutation(np.resize(levels, k // 32))).repeat(32)
    a = np.empty((k // 512, 16))
    for p in range(k // 512):
        a[p, :8] = np.random.permutation(np.resize(levels, 8))
        for g in range(8):
            far = levels[np.abs(levels - a[p, g]) >= 10]
            a[p, g + 8] = far[np.random.randint(len(far))]
    return np.exp2(a.ravel()).repeat(32)


BF16 = ml_dtypes.bfloat16


def bf(x):
    return np.asarray(x, np.float32).astype(BF16)


def f64(x):
    return np.asarray(x).astype(np.float64)


M, SP, H, FF, NH = 512, 384, 1024, 2560, 8
EPS = 1.1920929e-07


def rms_norm(x, w):
    var = np.mean(np.square(x), axis=-1, keepdims=True)
    return x * (1.0 / np.sqrt(var + EPS)) * w


def setup_inputs():
    s = mx_kscale(H)
    return {"x": bf(np.random.standard_normal((M, H))),
            "W_qkv": bf(np.random.standard_normal((2, H, 3 * H)) * 1.25 / np.sqrt(H) / s[None, :, None]),
            "ln1": bf((1.0 + 0.1 * np.random.standard_normal((2, H))) * s)}


def reference(x, W_qkv, ln1):
    x, W_qkv, ln1 = f64(x), f64(W_qkv), f64(ln1)
    h0 = rms_norm(x[:SP], ln1[0])
    h1 = rms_norm(x[SP:], ln1[1])
    y0 = mxq(h0, 1, "e4m3") @ mxq(W_qkv[0], 0, "e4m3")
    y1 = mxq(h1, 1, "e4m3") @ mxq(W_qkv[1], 0, "e4m3")
    return np.concatenate([y0, y1], axis=0)

@@ -1,0 +1,226 @@
+from contextlib import ExitStack
+
+import concourse.mybir as mybir
+from concourse.masks import make_identity
+
+F32 = mybir.dt.float32
+BF16 = mybir.dt.bfloat16
+I32 = mybir.dt.int32
+U32 = mybir.dt.uint32
+U8 = mybir.dt.uint8
+FP8X4 = mybir.dt.float8_e4m3fn_x4
+ALU = mybir.AluOpType
+ACT = mybir.ActivationFunctionType
+
+P = 128
+PACK = 4
+K_PASS = P * PACK
+ROWS, SPLIT, H, N_OUT = 512, 384, 1024, 3072
+EPS = 1.1920929e-07
+MODELS = 2
+PASSES = H // K_PASS
+K_BLOCKS = H // P
+ROW_TILES = ROWS // P
+FIRST_ROW_TILE = (0, SPLIT // P)
+N_ROW_TILES = (SPLIT // P, (ROWS - SPLIT) // P)
+BANK = 512
+CHUNK = 1024
+UNITS = N_OUT // CHUNK
+N_CHUNKS = MODELS * PASSES * UNITS
+BANKS_PER_CHUNK = CHUNK // BANK
+BASE_COLS = 624
+COLS_PER_BANK = 56
+
+FLOPS = 2 * ROWS * H * N_OUT
+
+
+def tile_twomodelblockrouted_pa_kernel(tc, x, W_qkv, ln1, out):
+    nc = tc.nc
+    with ExitStack() as ctx:
+        ctx.enter_context(tc.manual_schedule())
+        consts = ctx.enter_context(tc.tile_pool(name="consts", bufs=1))
+        rows_pool = ctx.enter_context(tc.tile_pool(name="rows", bufs=2))
+        small = ctx.enter_context(tc.tile_pool(name="small", bufs=ROW_TILES))
+        weights = ctx.enter_context(tc.tile_pool(name="weights", bufs=MODELS * PASSES))
+        grouped_pool = ctx.enter_context(tc.tile_pool(name="grouped", bufs=3))
+        quantised = ctx.enter_context(tc.tile_pool(name="quantised", bufs=6))
+        results = ctx.enter_context(tc.tile_pool(name="results", bufs=UNITS))
+
+        gain_rows = consts.tile([P, MODELS * H], BF16)
+        nc.vector.memset(gain_rows[:].bitcast(I32), 0)
+        eps = consts.tile([P, 1], F32)
+        nc.vector.memset(eps[:], EPS)
+        ones = consts.tile([P, P], BF16)
+        nc.vector.memset(ones[:], 1.0)
+        identity = consts.tile([P, P], BF16)
+        make_identity(nc, identity[:])
+        warm = consts.tile([P, 1], F32)
+        nc.scalar.activation(out=warm[:], in_=eps[:], func=ACT.Sqrt)
+
+        x_rows = []
+        for m in range(ROW_TILES):
+            x_m = rows_pool.tile([P, H], BF16, name="x_rows", bufs=ROW_TILES)
+            nc.sync.dma_start(out=x_m[:], in_=x[m * P : (m + 1) * P, :])
+            x_rows.append(x_m)
+            if m == 0:
+                nc.sync.dma_start(
+                    out=gain_rows[0:1, :], in_=ln1.rearrange("(o g) k -> o (g k)", o=1)
+                )
+        w_raw = []
+        for g in range(MODELS):
+            for c in range(PASSES):
+                raw = weights.tile([P, PACK, N_OUT], BF16, name="w_raw")
+                nc.sync.dma_start(
+                    out=raw[:],
+                    in_=W_qkv[g, c * K_PASS : (c + 1) * K_PASS, :].rearrange("(p t) n -> p t n", t=PACK),
+                )
+                w_raw.append(raw)
+
+        h_grouped = consts.tile([P, ROW_TILES, PASSES, P, PACK], BF16, align_bytes=64)
+        h_codes = consts.tile([P, ROW_TILES, PASSES, P], U32, align_bytes=64)
+        h_scales = consts.tile([P, ROW_TILES, PASSES, P], U8, align_bytes=64)
+        with tc.psum_pool(name="head_psum", bufs=4) as head_psum:
+            gains = []
+            for s in range(MODELS * PASSES):
+                gains_s = head_psum.tile([P, BANK], F32, name="gains")
+                nc.tensor.matmul(
+                    out=gains_s[:],
+                    lhsT=ones[:],
+                    rhs=gain_rows[:, s * BANK : (s + 1) * BANK],
+                    start=True,
+                    stop=True,
+                )
+                gains.append(gains_s)
+            sum_sq = []
+            h_t = []
+
+            def sum_squares(m):
+                squares = rows_pool.tile([P, H], BF16, name="squares")
+                sum_sq.append(small.tile([P, 1], F32, name="sum_sq"))
+                nc.scalar.activation(
+                    out=squares[:], in_=x_rows[m][:], func=ACT.Square, accum_out=sum_sq[m][:]
+                )
+
+            def normalise_and_transpose(m):
+                g = 0 if m < FIRST_ROW_TILE[1] else 1
+                rms = small.tile([P, 1], F32, name="rms")
+                nc.scalar.activation(
+                    out=rms[:], in_=sum_sq[m][:], func=ACT.Sqrt, scale=1.0 / H, bias=eps[:]
+                )
+                rstd = small.tile([P, 1], F32, name="rstd")
+                nc.vector.reciprocal(out=rstd[:], in_=rms[:])
+                h_m = rows_pool.tile([P, H], BF16, name="h_rows")
+                for c in range(PASSES):
+                    pass_cols = slice(c * K_PASS, (c + 1) * K_PASS)
+                    nc.vector.scalar_tensor_tensor(
+                        out=h_m[:, pass_cols].rearrange("p (t q) -> p t q", t=PACK),
+                        in0=x_rows[m][:, pass_cols].rearrange("p (q t) -> p t q", t=PACK),
+                        scalar=rstd[:],
+                        in1=gains[g * PASSES + c][:].rearrange("p (q t) -> p t q", t=PACK),
+                        op0=ALU.mult,
+                        op1=ALU.mult,
+                    )
+                h_t.append(head_psum.tile([P, K_BLOCKS, P], BF16, name="h_t"))
+                for b in range(K_BLOCKS):
+                    nc.tensor.transpose(h_t[m][:, b, :], h_m[:, b * P : (b + 1) * P], identity[:])
+
+            sum_squares(0)
+            for m in range(1, ROW_TILES):
+                sum_squares(m)
+                normalise_and_transpose(m - 1)
+            normalise_and_transpose(ROW_TILES - 1)
+            for m in range(ROW_TILES):
+                nc.scalar.copy(
+                    out=h_grouped[:, m],
+                    in_=h_t[m][:].rearrange("p (c t) r -> p c r t", t=PACK),
+                )
+
+        acc_psum = ctx.enter_context(tc.psum_pool(name="acc_psum", bufs=8))
+        w_grouped = {}
+        w_codes = {}
+        w_scales = {}
+        acc = {}
+
+        def completes_columns(i):
+            return 0 <= i < N_CHUNKS and (i // UNITS) % PASSES == PASSES - 1
+
+        def banks_of(i):
+            return BANKS_PER_CHUNK * N_ROW_TILES[i // (PASSES * UNITS)] if completes_columns(i) else 0
+
+        def regroup(i, vector_cols):
+            raw = w_raw[i // UNITS]
+            first = (i % UNITS) * CHUNK
+            grouped = grouped_pool.tile([P, CHUNK, PACK], BF16, name="w_grouped", align_bytes=64)
+            nc.vector.tensor_copy(
+                out=grouped[:, 0:vector_cols, :].rearrange("p (w i) t -> p w t i", i=4),
+                in_=raw[:, :, first : first + vector_cols].rearrange("p t (w i) -> p w t i", i=4),
+            )
+            if vector_cols < CHUNK:
+                nc.scalar.copy(
+                    out=grouped[:, vector_cols:CHUNK, :].rearrange("p (w i) t -> p w t i", i=4),
+                    in_=raw[:, :, first + vector_cols : first + CHUNK].rearrange(
+                        "p t (w i) -> p w t i", i=4
+                    ),
+                )
+            w_grouped[i] = grouped
+
+        def quantise(i):
+            w_codes[i] = quantised.tile([P, CHUNK], U32, name="w_codes", align_bytes=64)
+            w_scales[i] = quantised.tile([P, CHUNK], U8, name="w_scales", align_bytes=64)
+            nc.vector.quantize_mx(
+                out=w_codes[i][:].bitcast(FP8X4),
+                scales=w_scales[i][:],
+                in_=w_grouped[i][:].rearrange("p w t -> p (w t)"),
+            )
+
+        def multiply(i):
+            g = i // (PASSES * UNITS)
+            for n in range(BANKS_PER_CHUNK):
+                n_cols = slice(n * BANK, (n + 1) * BANK)
+                for r in range(N_ROW_TILES[g]):
+                    m = FIRST_ROW_TILE[g] + r
+                    acc[(i, n, r)] = acc_psum.tile([P, BANK], F32, name="acc")
+                    for c in range(PASSES):
+                        chunk = i - (PASSES - 1 - c) * UNITS
+                        nc.tensor.matmul_mx(
+                            out=acc[(i, n, r)][:],
+                            lhsT=h_codes[:, m, c, :].bitcast(FP8X4),
+                            lhsT_scale=h_scales[:, m, c, :],
+                            rhs=w_codes[chunk][:, n_cols].bitcast(FP8X4),
+                            rhs_scale=w_scales[chunk][:, n_cols],
+                            start=(c == 0),
+                            stop=(c == PASSES - 1),
+                        )
+
+        def empty_and_store(i):
+            g, u = i // (PASSES * UNITS), i % UNITS
+            out_rows = results.tile([P, N_ROW_TILES[g], CHUNK], F32, name="out_rows%d" % g)
+            for n in range(BANKS_PER_CHUNK):
+                for r in range(N_ROW_TILES[g]):
+                    nc.scalar.copy(
+                        out=out_rows[:, r, n * BANK : (n + 1) * BANK], in_=acc[(i, n, r)][:]
+                    )
+            first_row = FIRST_ROW_TILE[g] * P
+            nc.sync.dma_start(
+                out=out[
+                    first_row : first_row + N_ROW_TILES[g] * P, u * CHUNK : (u + 1) * CHUNK
+                ].rearrange("(r p) n -> p r n", p=P),
+                in_=out_rows[:],
+            )
+
+        for s in range(N_CHUNKS + 3):
+            if s < N_CHUNKS:
+                regroup(s, min(CHUNK, BASE_COLS + COLS_PER_BANK * banks_of(s - 3)))
+            if s == 1:
+                for m in range(ROW_TILES):
+                    nc.vector.quantize_mx(
+                        out=h_codes[:, m].rearrange("p c r -> p (c r)").bitcast(FP8X4),
+                        scales=h_scales[:, m].rearrange("p c r -> p (c r)"),
+                        in_=h_grouped[:, m].rearrange("p c r t -> p (c r t)"),
+                    )
+            if 0 <= s - 1 < N_CHUNKS:
+                quantise(s - 1)
+            if completes_columns(s - 3):
+                empty_and_store(s - 3)
+            if completes_columns(s - 2):
+                multiply(s - 2)

@@ -5,7 +5,6 @@ from concourse.masks import make_identity
 
 F32 = mybir.dt.float32
 BF16 = mybir.dt.bfloat16
-I32 = mybir.dt.int32
 U32 = mybir.dt.uint32
 U8 = mybir.dt.uint8
 FP8X4 = mybir.dt.float8_e4m3fn_x4
@@ -19,7 +18,6 @@ ROWS, SPLIT, H, N_OUT = 512, 384, 1024, 3072
 EPS = 1.1920929e-07
 MODELS = 2
 PASSES = H // K_PASS
-K_BLOCKS = H // P
 ROW_TILES = ROWS // P
 FIRST_ROW_TILE = (0, SPLIT // P)
 N_ROW_TILES = (SPLIT // P, (ROWS - SPLIT) // P)
@@ -27,9 +25,11 @@ BANK = 512
 CHUNK = 1024
 UNITS = N_OUT // CHUNK
 N_CHUNKS = MODELS * PASSES * UNITS
+LAST_CHUNK = N_CHUNKS - 1
 BANKS_PER_CHUNK = CHUNK // BANK
-BASE_COLS = 624
-COLS_PER_BANK = 56
+BASE_COLS = 512
+COLS_PER_BANK = 84
+HEAD_COLS = (0, 160)
 
 FLOPS = 2 * ROWS * H * N_OUT
 
@@ -43,16 +43,13 @@ def tile_twomodelblockrouted_pa_kernel(tc, x, W_qkv, ln1, out):
         small = ctx.enter_context(tc.tile_pool(name="small", bufs=ROW_TILES))
         weights = ctx.enter_context(tc.tile_pool(name="weights", bufs=MODELS * PASSES))
         grouped_pool = ctx.enter_context(tc.tile_pool(name="grouped", bufs=3))
-        quantised = ctx.enter_context(tc.tile_pool(name="quantised", bufs=6))
+        quantised = ctx.enter_context(tc.tile_pool(name="quantised", bufs=5))
         results = ctx.enter_context(tc.tile_pool(name="results", bufs=UNITS))
 
-        gain_rows = consts.tile([P, MODELS * H], BF16)
-        nc.vector.memset(gain_rows[:].bitcast(I32), 0)
+        gains = consts.tile([P, MODELS * PASSES, PACK], BF16)
         eps = consts.tile([P, 1], F32)
         nc.vector.memset(eps[:], EPS)
-        ones = consts.tile([P, P], BF16)
-        nc.vector.memset(ones[:], 1.0)
-        identity = consts.tile([P, P], BF16)
+        identity = consts.tile([P, P], F32)
         make_identity(nc, identity[:])
         warm = consts.tile([P, 1], F32)
         nc.scalar.activation(out=warm[:], in_=eps[:], func=ACT.Sqrt)
@@ -64,153 +61,161 @@ def tile_twomodelblockrouted_pa_kernel(tc, x, W_qkv, ln1, out):
             x_rows.append(x_m)
             if m == 0:
                 nc.sync.dma_start(
-                    out=gain_rows[0:1, :], in_=ln1.rearrange("(o g) k -> o (g k)", o=1)
+                    out=gains[:],
+                    in_=ln1.rearrange("g k -> (g k)").rearrange("(s p t) -> p s t", p=P, t=PACK),
                 )
-        w_raw = []
-        for g in range(MODELS):
+        w_raw = {}
+        for g, first_unit, units in ((0, 0, 1), (0, 1, 1), (0, 2, 1), (1, 0, 1), (1, 1, 2)):
             for c in range(PASSES):
-                raw = weights.tile([P, PACK, N_OUT], BF16, name="w_raw")
+                width = units * CHUNK
+                raw = weights.tile(
+                    [P, PACK, width], BF16, name="w_raw%d" % units, bufs=8 if units == 1 else PASSES
+                )
                 nc.sync.dma_start(
                     out=raw[:],
-                    in_=W_qkv[g, c * K_PASS : (c + 1) * K_PASS, :].rearrange("(p t) n -> p t n", t=PACK),
+                    in_=W_qkv[
+                        g, c * K_PASS : (c + 1) * K_PASS, first_unit * CHUNK : first_unit * CHUNK + width
+                    ].rearrange("(p t) n -> p t n", t=PACK),
                 )
-                w_raw.append(raw)
+                for u in range(units):
+                    w_raw[(g, c, first_unit + u)] = raw[:, :, u * CHUNK : (u + 1) * CHUNK]
 
         h_grouped = consts.tile([P, ROW_TILES, PASSES, P, PACK], BF16, align_bytes=64)
         h_codes = consts.tile([P, ROW_TILES, PASSES, P], U32, align_bytes=64)
         h_scales = consts.tile([P, ROW_TILES, PASSES, P], U8, align_bytes=64)
-        with tc.psum_pool(name="head_psum", bufs=4) as head_psum:
-            gains = []
-            for s in range(MODELS * PASSES):
-                gains_s = head_psum.tile([P, BANK], F32, name="gains")
-                nc.tensor.matmul(
-                    out=gains_s[:],
-                    lhsT=ones[:],
-                    rhs=gain_rows[:, s * BANK : (s + 1) * BANK],
-                    start=True,
-                    stop=True,
-                )
-                gains.append(gains_s)
+        with tc.psum_pool(name="head_psum", bufs=8) as head_psum:
             sum_sq = []
-            h_t = []
+            x_t = {}
 
             def sum_squares(m):
-                squares = rows_pool.tile([P, H], BF16, name="squares")
+                squares = rows_pool.tile([P, H], BF16, name="squares", bufs=1)
                 sum_sq.append(small.tile([P, 1], F32, name="sum_sq"))
                 nc.scalar.activation(
                     out=squares[:], in_=x_rows[m][:], func=ACT.Square, accum_out=sum_sq[m][:]
                 )
 
-            def normalise_and_transpose(m):
-                g = 0 if m < FIRST_ROW_TILE[1] else 1
+            def scale_and_transpose(m):
                 rms = small.tile([P, 1], F32, name="rms")
                 nc.scalar.activation(
                     out=rms[:], in_=sum_sq[m][:], func=ACT.Sqrt, scale=1.0 / H, bias=eps[:]
                 )
                 rstd = small.tile([P, 1], F32, name="rstd")
                 nc.vector.reciprocal(out=rstd[:], in_=rms[:])
-                h_m = rows_pool.tile([P, H], BF16, name="h_rows")
+                scaled = rows_pool.tile([P, PASSES, PACK, P], F32, name="scaled")
                 for c in range(PASSES):
-                    pass_cols = slice(c * K_PASS, (c + 1) * K_PASS)
-                    nc.vector.scalar_tensor_tensor(
-                        out=h_m[:, pass_cols].rearrange("p (t q) -> p t q", t=PACK),
-                        in0=x_rows[m][:, pass_cols].rearrange("p (q t) -> p t q", t=PACK),
-                        scalar=rstd[:],
-                        in1=gains[g * PASSES + c][:].rearrange("p (q t) -> p t q", t=PACK),
-                        op0=ALU.mult,
-                        op1=ALU.mult,
+                    nc.vector.tensor_scalar_mul(
+                        out=scaled[:, c],
+                        in0=x_rows[m][:, c * K_PASS : (c + 1) * K_PASS].rearrange("p (q t) -> p t q", t=PACK),
+                        scalar1=rstd[:],
                     )
-                h_t.append(head_psum.tile([P, K_BLOCKS, P], BF16, name="h_t"))
-                for b in range(K_BLOCKS):
-                    nc.tensor.transpose(h_t[m][:, b, :], h_m[:, b * P : (b + 1) * P], identity[:])
+                for c in range(PASSES):
+                    x_t[(m, c)] = head_psum.tile([P, PACK, P], F32, name="x_t")
+                    for t in range(PACK):
+                        nc.tensor.transpose(x_t[(m, c)][:, t, :], scaled[:, c, t, :], identity[:])
+
+            def multiply_by_gains(m):
+                g = 0 if m < FIRST_ROW_TILE[1] else 1
+                for c in range(PASSES):
+                    nc.vector.tensor_tensor(
+                        out=h_grouped[:, m, c],
+                        in0=x_t[(m, c)][:].rearrange("p t r -> p r t"),
+                        in1=gains[:, g * PASSES + c, :].unsqueeze(1).to_broadcast([P, P, PACK]),
+                        op=ALU.mult,
+                    )
 
             sum_squares(0)
-            for m in range(1, ROW_TILES):
-                sum_squares(m)
-                normalise_and_transpose(m - 1)
-            normalise_and_transpose(ROW_TILES - 1)
             for m in range(ROW_TILES):
-                nc.scalar.copy(
-                    out=h_grouped[:, m],
-                    in_=h_t[m][:].rearrange("p (c t) r -> p c r t", t=PACK),
-                )
+                if m + 1 < ROW_TILES:
+                    sum_squares(m + 1)
+                scale_and_transpose(m)
+                if m > 0:
+                    multiply_by_gains(m - 1)
+            multiply_by_gains(ROW_TILES - 1)
 
         acc_psum = ctx.enter_context(tc.psum_pool(name="acc_psum", bufs=8))
         w_grouped = {}
         w_codes = {}
         w_scales = {}
         acc = {}
+        out_rows = {}
 
-        def completes_columns(i):
-            return 0 <= i < N_CHUNKS and (i // UNITS) % PASSES == PASSES - 1
+        def place(i):
+            return i // (PASSES * UNITS), i % PASSES, (i // PASSES) % UNITS
 
-        def banks_of(i):
-            return BANKS_PER_CHUNK * N_ROW_TILES[i // (PASSES * UNITS)] if completes_columns(i) else 0
+        def bank_group(s):
+            i, n = (s - 2, 0) if s % PASSES == 1 else (s - 3, 1)
+            return (i, n) if 0 < i < N_CHUNKS else None
+
+        def banks_in_step(s):
+            group = bank_group(s)
+            return N_ROW_TILES[place(group[0])[0]] if group else 0
 
         def regroup(i, vector_cols):
-            raw = w_raw[i // UNITS]
-            first = (i % UNITS) * CHUNK
+            g, c, u = place(i)
+            raw = w_raw[(g, c, u)]
             grouped = grouped_pool.tile([P, CHUNK, PACK], BF16, name="w_grouped", align_bytes=64)
-            nc.vector.tensor_copy(
-                out=grouped[:, 0:vector_cols, :].rearrange("p (w i) t -> p w t i", i=4),
-                in_=raw[:, :, first : first + vector_cols].rearrange("p t (w i) -> p w t i", i=4),
-            )
-            if vector_cols < CHUNK:
-                nc.scalar.copy(
-                    out=grouped[:, vector_cols:CHUNK, :].rearrange("p (w i) t -> p w t i", i=4),
-                    in_=raw[:, :, first + vector_cols : first + CHUNK].rearrange(
-                        "p t (w i) -> p w t i", i=4
-                    ),
+            if vector_cols:
+                nc.vector.tensor_copy(
+                    out=grouped[:, 0:vector_cols, :].rearrange("p (w i) t -> p w t i", i=4),
+                    in_=raw[:, :, 0:vector_cols].rearrange("p t (w i) -> p w t i", i=4),
                 )
+            nc.scalar.copy(
+                out=grouped[:, vector_cols:CHUNK, :].rearrange("p (w i) t -> p w t i", i=4),
+                in_=raw[:, :, vector_cols:CHUNK].rearrange("p t (w i) -> p w t i", i=4),
+            )
             w_grouped[i] = grouped
 
-        def quantise(i):
-            w_codes[i] = quantised.tile([P, CHUNK], U32, name="w_codes", align_bytes=64)
-            w_scales[i] = quantised.tile([P, CHUNK], U8, name="w_scales", align_bytes=64)
+        def quantise(i, first, width):
+            if first == 0:
+                w_codes[i] = quantised.tile([P, CHUNK], U32, name="w_codes", align_bytes=64)
+                w_scales[i] = quantised.tile([P, CHUNK], U8, name="w_scales", align_bytes=64)
             nc.vector.quantize_mx(
-                out=w_codes[i][:].bitcast(FP8X4),
-                scales=w_scales[i][:],
-                in_=w_grouped[i][:].rearrange("p w t -> p (w t)"),
+                out=w_codes[i][:, first : first + width].bitcast(FP8X4),
+                scales=w_scales[i][:, first : first + width],
+                in_=w_grouped[i][:, first : first + width, :].rearrange("p w t -> p (w t)"),
             )
 
-        def multiply(i):
-            g = i // (PASSES * UNITS)
-            for n in range(BANKS_PER_CHUNK):
-                n_cols = slice(n * BANK, (n + 1) * BANK)
-                for r in range(N_ROW_TILES[g]):
-                    m = FIRST_ROW_TILE[g] + r
-                    acc[(i, n, r)] = acc_psum.tile([P, BANK], F32, name="acc")
-                    for c in range(PASSES):
-                        chunk = i - (PASSES - 1 - c) * UNITS
-                        nc.tensor.matmul_mx(
-                            out=acc[(i, n, r)][:],
-                            lhsT=h_codes[:, m, c, :].bitcast(FP8X4),
-                            lhsT_scale=h_scales[:, m, c, :],
-                            rhs=w_codes[chunk][:, n_cols].bitcast(FP8X4),
-                            rhs_scale=w_scales[chunk][:, n_cols],
-                            start=(c == 0),
-                            stop=(c == PASSES - 1),
-                        )
-
-        def empty_and_store(i):
-            g, u = i // (PASSES * UNITS), i % UNITS
-            out_rows = results.tile([P, N_ROW_TILES[g], CHUNK], F32, name="out_rows%d" % g)
-            for n in range(BANKS_PER_CHUNK):
-                for r in range(N_ROW_TILES[g]):
-                    nc.scalar.copy(
-                        out=out_rows[:, r, n * BANK : (n + 1) * BANK], in_=acc[(i, n, r)][:]
+        def multiply(i, n):
+            g = place(i)[0]
+            n_cols = slice(n * BANK, (n + 1) * BANK)
+            for r in range(N_ROW_TILES[g]):
+                m = FIRST_ROW_TILE[g] + r
+                acc[(i, n, r)] = acc_psum.tile([P, BANK], F32, name="acc")
+                for c in range(PASSES):
+                    chunk = i - (PASSES - 1 - c)
+                    nc.tensor.matmul_mx(
+                        out=acc[(i, n, r)][:],
+                        lhsT=h_codes[:, m, c, :].bitcast(FP8X4),
+                        lhsT_scale=h_scales[:, m, c, :],
+                        rhs=w_codes[chunk][:, n_cols].bitcast(FP8X4),
+                        rhs_scale=w_scales[chunk][:, n_cols],
+                        start=(c == 0),
+                        stop=(c == PASSES - 1),
                     )
+
+        def empty(i, n):
+            g = place(i)[0]
+            if n == 0:
+                out_rows[i] = results.tile([P, N_ROW_TILES[g], CHUNK], F32, name="out_rows%d" % g)
+            for r in range(N_ROW_TILES[g]):
+                nc.scalar.copy(
+                    out=out_rows[i][:, r, n * BANK : (n + 1) * BANK], in_=acc[(i, n, r)][:]
+                )
+
+        def store(i, first, width):
+            g, c, u = place(i)
             first_row = FIRST_ROW_TILE[g] * P
             nc.sync.dma_start(
                 out=out[
-                    first_row : first_row + N_ROW_TILES[g] * P, u * CHUNK : (u + 1) * CHUNK
+                    first_row : first_row + N_ROW_TILES[g] * P,
+                    u * CHUNK + first : u * CHUNK + first + width,
                 ].rearrange("(r p) n -> p r n", p=P),
-                in_=out_rows[:],
+                in_=out_rows[i][:, :, first : first + width],
             )
 
         for s in range(N_CHUNKS + 3):
             if s < N_CHUNKS:
-                regroup(s, min(CHUNK, BASE_COLS + COLS_PER_BANK * banks_of(s - 3)))
+                regroup(s, HEAD_COLS[s] if s < len(HEAD_COLS) else BASE_COLS + COLS_PER_BANK * banks_in_step(s))
             if s == 1:
                 for m in range(ROW_TILES):
                     nc.vector.quantize_mx(
@@ -218,9 +223,19 @@ def tile_twomodelblockrouted_pa_kernel(tc, x, W_qkv, ln1, out):
                         scales=h_scales[:, m].rearrange("p c r -> p (c r)"),
                         in_=h_grouped[:, m].rearrange("p c r t -> p (c r t)"),
                     )
-            if 0 <= s - 1 < N_CHUNKS:
-                quantise(s - 1)
-            if completes_columns(s - 3):
-                empty_and_store(s - 3)
-            if completes_columns(s - 2):
-                multiply(s - 2)
+            if 0 <= s - 1 < LAST_CHUNK:
+                quantise(s - 1, 0, CHUNK)
+                if place(s - 1)[1] == PASSES - 1:
+                    for n in range(BANKS_PER_CHUNK):
+                        multiply(s - 1, n)
+            if s - 1 == LAST_CHUNK:
+                for n in range(BANKS_PER_CHUNK):
+                    quantise(LAST_CHUNK, n * BANK, BANK)
+                    multiply(LAST_CHUNK, n)
+            group = bank_group(s)
+            if group:
+                empty(group[0], group[1])
+                if group[0] == LAST_CHUNK:
+                    store(group[0], group[1] * BANK, BANK)
+                elif group[1] == BANKS_PER_CHUNK - 1:
+                    store(group[0], 0, CHUNK)

@@ -5,6 +5,7 @@ from concourse.masks import make_identity
 
 F32 = mybir.dt.float32
 BF16 = mybir.dt.bfloat16
+I32 = mybir.dt.int32
 U32 = mybir.dt.uint32
 U8 = mybir.dt.uint8
 FP8X4 = mybir.dt.float8_e4m3fn_x4
@@ -47,10 +48,14 @@ def tile_twomodelblockrouted_pa_kernel(tc, x, W_qkv, ln1, out):
         results = ctx.enter_context(tc.tile_pool(name="results", bufs=UNITS))
 
         gains = consts.tile([P, MODELS * PASSES, PACK], BF16)
+        gain_rows = consts.tile([P, K_PASS], BF16)
+        nc.vector.memset(gain_rows[:].bitcast(I32), 0)
         eps = consts.tile([P, 1], F32)
         nc.vector.memset(eps[:], EPS)
         identity = consts.tile([P, P], F32)
         make_identity(nc, identity[:])
+        identity_bf16 = consts.tile([P, P], BF16)
+        nc.vector.tensor_copy(out=identity_bf16[:], in_=identity[:])
         warm = consts.tile([P, 1], F32)
         nc.scalar.activation(out=warm[:], in_=eps[:], func=ACT.Sqrt)
 
@@ -61,8 +66,8 @@ def tile_twomodelblockrouted_pa_kernel(tc, x, W_qkv, ln1, out):
             x_rows.append(x_m)
             if m == 0:
                 nc.sync.dma_start(
-                    out=gains[:],
-                    in_=ln1.rearrange("g k -> (g k)").rearrange("(s p t) -> p s t", p=P, t=PACK),
+                    out=gain_rows[0 : MODELS * PASSES, :],
+                    in_=ln1.rearrange("g (c k) -> (g c) k", c=PASSES),
                 )
         w_raw = {}
         for g, first_unit, units in ((0, 0, 1), (0, 1, 1), (0, 2, 1), (1, 0, 1), (1, 1, 2)):
@@ -84,6 +89,12 @@ def tile_twomodelblockrouted_pa_kernel(tc, x, W_qkv, ln1, out):
         h_codes = consts.tile([P, ROW_TILES, PASSES, P], U32, align_bytes=64)
         h_scales = consts.tile([P, ROW_TILES, PASSES, P], U8, align_bytes=64)
         with tc.psum_pool(name="head_psum", bufs=8) as head_psum:
+            gains_t = head_psum.tile([P, PACK, P], BF16, name="x_t")
+            for t in range(PACK):
+                nc.tensor.transpose(gains_t[:, t, :], gain_rows[:, t:K_PASS:PACK], identity_bf16[:])
+            nc.vector.tensor_copy(
+                out=gains[:], in_=gains_t[:, :, 0 : MODELS * PASSES].rearrange("p t s -> p s t")
+            )
             sum_sq = []
             x_t = {}
 

@@ -29,7 +29,7 @@ N_CHUNKS = MODELS * PASSES * UNITS
 LAST_CHUNK = N_CHUNKS - 1
 BANKS_PER_CHUNK = CHUNK // BANK
 BASE_COLS = 512
-COLS_PER_BANK = 84
+COLS_PER_BANK = 80
 HEAD_COLS = (0, 160)
 
 FLOPS = 2 * ROWS * H * N_OUT
@@ -92,26 +92,37 @@ def tile_twomodelblockrouted_pa_kernel(tc, x, W_qkv, ln1, out):
             gains_t = head_psum.tile([P, PACK, P], BF16, name="x_t")
             for t in range(PACK):
                 nc.tensor.transpose(gains_t[:, t, :], gain_rows[:, t:K_PASS:PACK], identity_bf16[:])
-            nc.vector.tensor_copy(
-                out=gains[:], in_=gains_t[:, :, 0 : MODELS * PASSES].rearrange("p t s -> p s t")
-            )
             sum_sq = []
+            rms = []
             x_t = {}
 
             def sum_squares(m):
-                squares = rows_pool.tile([P, H], BF16, name="squares", bufs=1)
                 sum_sq.append(small.tile([P, 1], F32, name="sum_sq"))
+                squares = rows_pool.tile([P, H], BF16, name="squares%d" % (m == 1), bufs=1)
+                if m == 1:
+                    nc.vector.scalar_tensor_tensor(
+                        out=squares[:],
+                        in0=x_rows[m][:],
+                        scalar=1.0,
+                        in1=x_rows[m][:],
+                        op0=ALU.mult,
+                        op1=ALU.mult,
+                        accum_out=sum_sq[m][:],
+                    )
+                else:
+                    nc.scalar.activation(
+                        out=squares[:], in_=x_rows[m][:], func=ACT.Square, accum_out=sum_sq[m][:]
+                    )
+
+            def root(m):
+                rms.append(small.tile([P, 1], F32, name="rms"))
                 nc.scalar.activation(
-                    out=squares[:], in_=x_rows[m][:], func=ACT.Square, accum_out=sum_sq[m][:]
+                    out=rms[m][:], in_=sum_sq[m][:], func=ACT.Sqrt, scale=1.0 / H, bias=eps[:]
                 )
 
             def scale_and_transpose(m):
-                rms = small.tile([P, 1], F32, name="rms")
-                nc.scalar.activation(
-                    out=rms[:], in_=sum_sq[m][:], func=ACT.Sqrt, scale=1.0 / H, bias=eps[:]
-                )
                 rstd = small.tile([P, 1], F32, name="rstd")
-                nc.vector.reciprocal(out=rstd[:], in_=rms[:])
+                nc.vector.reciprocal(out=rstd[:], in_=rms[m][:])
                 scaled = rows_pool.tile([P, PASSES, PACK, P], F32, name="scaled")
                 for c in range(PASSES):
                     nc.vector.tensor_scalar_mul(
@@ -135,9 +146,16 @@ def tile_twomodelblockrouted_pa_kernel(tc, x, W_qkv, ln1, out):
                     )
 
             sum_squares(0)
+            sum_squares(1)
+            root(0)
+            nc.vector.tensor_copy(
+                out=gains[:], in_=gains_t[:, :, 0 : MODELS * PASSES].rearrange("p t s -> p s t")
+            )
             for m in range(ROW_TILES):
+                if m + 2 < ROW_TILES:
+                    sum_squares(m + 2)
                 if m + 1 < ROW_TILES:
-                    sum_squares(m + 1)
+                    root(m + 1)
                 scale_and_transpose(m)
                 if m > 0:
                     multiply_by_gains(m - 1)

@@ -28,9 +28,12 @@ UNITS = N_OUT // CHUNK
 N_CHUNKS = MODELS * PASSES * UNITS
 LAST_CHUNK = N_CHUNKS - 1
 BANKS_PER_CHUNK = CHUNK // BANK
-BASE_COLS = 512
+BASE_COLS = 448
 COLS_PER_BANK = 80
-HEAD_COLS = (0, 160)
+HEAD_COLS = (0, 128)
+PE_CHUNKS = range(2, 11)
+PE_COLS = 256
+PE_MATMUL_COLS = BANK // PACK
 
 FLOPS = 2 * ROWS * H * N_OUT
 
@@ -161,7 +164,8 @@ def tile_twomodelblockrouted_pa_kernel(tc, x, W_qkv, ln1, out):
                     multiply_by_gains(m - 1)
             multiply_by_gains(ROW_TILES - 1)
 
-        acc_psum = ctx.enter_context(tc.psum_pool(name="acc_psum", bufs=8))
+        acc_psum = ctx.enter_context(tc.psum_pool(name="acc_psum", bufs=6))
+        turn_psum = ctx.enter_context(tc.psum_pool(name="turn_psum", bufs=2))
         w_grouped = {}
         w_codes = {}
         w_scales = {}
@@ -188,10 +192,26 @@ def tile_twomodelblockrouted_pa_kernel(tc, x, W_qkv, ln1, out):
                     out=grouped[:, 0:vector_cols, :].rearrange("p (w i) t -> p w t i", i=4),
                     in_=raw[:, :, 0:vector_cols].rearrange("p t (w i) -> p w t i", i=4),
                 )
+            direct_end = CHUNK
+            if i in PE_CHUNKS:
+                direct_end = CHUNK - PE_COLS
+                turned = turn_psum.tile([P, PE_COLS, PACK], BF16, name="turned")
+                for a in range(0, PE_COLS, PE_MATMUL_COLS):
+                    nc.tensor.matmul(
+                        out=turned[:, a : a + PE_MATMUL_COLS, :],
+                        lhsT=identity_bf16[:],
+                        rhs=raw[:, :, direct_end + a : direct_end + a + PE_MATMUL_COLS].rearrange(
+                            "p t w -> p w t"
+                        ),
+                        start=True,
+                        stop=True,
+                    )
             nc.scalar.copy(
-                out=grouped[:, vector_cols:CHUNK, :].rearrange("p (w i) t -> p w t i", i=4),
-                in_=raw[:, :, vector_cols:CHUNK].rearrange("p t (w i) -> p w t i", i=4),
+                out=grouped[:, vector_cols:direct_end, :].rearrange("p (w i) t -> p w t i", i=4),
+                in_=raw[:, :, vector_cols:direct_end].rearrange("p t (w i) -> p w t i", i=4),
             )
+            if i in PE_CHUNKS:
+                nc.scalar.copy(out=grouped[:, direct_end:CHUNK, :], in_=turned[:])
             w_grouped[i] = grouped
 
         def quantise(i, first, width):

@@ -166,6 +166,7 @@ def tile_twomodelblockrouted_pa_kernel(tc, x, W_qkv, ln1, out):
 
         acc_psum = ctx.enter_context(tc.psum_pool(name="acc_psum", bufs=6))
         turn_psum = ctx.enter_context(tc.psum_pool(name="turn_psum", bufs=2))
+        turned = {}
         w_grouped = {}
         w_codes = {}
         w_scales = {}
@@ -183,6 +184,18 @@ def tile_twomodelblockrouted_pa_kernel(tc, x, W_qkv, ln1, out):
             group = bank_group(s)
             return N_ROW_TILES[place(group[0])[0]] if group else 0
 
+        def turn(i):
+            turned[i] = turn_psum.tile([P, PE_COLS, PACK], BF16, name="turned")
+            for a in range(0, PE_COLS, PE_MATMUL_COLS):
+                first = CHUNK - PE_COLS + a
+                nc.tensor.matmul(
+                    out=turned[i][:, a : a + PE_MATMUL_COLS, :],
+                    lhsT=identity_bf16[:],
+                    rhs=w_raw[place(i)][:, :, first : first + PE_MATMUL_COLS].rearrange("p t w -> p w t"),
+                    start=True,
+                    stop=True,
+                )
+
         def regroup(i, vector_cols):
             g, c, u = place(i)
             raw = w_raw[(g, c, u)]
@@ -192,26 +205,13 @@ def tile_twomodelblockrouted_pa_kernel(tc, x, W_qkv, ln1, out):
                     out=grouped[:, 0:vector_cols, :].rearrange("p (w i) t -> p w t i", i=4),
                     in_=raw[:, :, 0:vector_cols].rearrange("p t (w i) -> p w t i", i=4),
                 )
-            direct_end = CHUNK
-            if i in PE_CHUNKS:
-                direct_end = CHUNK - PE_COLS
-                turned = turn_psum.tile([P, PE_COLS, PACK], BF16, name="turned")
-                for a in range(0, PE_COLS, PE_MATMUL_COLS):
-                    nc.tensor.matmul(
-                        out=turned[:, a : a + PE_MATMUL_COLS, :],
-                        lhsT=identity_bf16[:],
-                        rhs=raw[:, :, direct_end + a : direct_end + a + PE_MATMUL_COLS].rearrange(
-                            "p t w -> p w t"
-                        ),
-                        start=True,
-                        stop=True,
-                    )
+            direct_end = CHUNK - PE_COLS if i in PE_CHUNKS else CHUNK
             nc.scalar.copy(
                 out=grouped[:, vector_cols:direct_end, :].rearrange("p (w i) t -> p w t i", i=4),
                 in_=raw[:, :, vector_cols:direct_end].rearrange("p t (w i) -> p w t i", i=4),
             )
             if i in PE_CHUNKS:
-                nc.scalar.copy(out=grouped[:, direct_end:CHUNK, :], in_=turned[:])
+                nc.scalar.copy(out=grouped[:, direct_end:CHUNK, :], in_=turned[i][:])
             w_grouped[i] = grouped
 
         def quantise(i, first, width):
@@ -274,9 +274,11 @@ def tile_twomodelblockrouted_pa_kernel(tc, x, W_qkv, ln1, out):
                     )
             if 0 <= s - 1 < LAST_CHUNK:
                 quantise(s - 1, 0, CHUNK)
-                if place(s - 1)[1] == PASSES - 1:
-                    for n in range(BANKS_PER_CHUNK):
-                        multiply(s - 1, n)
+            for n in range(BANKS_PER_CHUNK):
+                if s % PASSES == 0 and s + 1 + n in PE_CHUNKS:
+                    turn(s + 1 + n)
+                if 0 <= s - 1 < LAST_CHUNK and place(s - 1)[1] == PASSES - 1:
+                    multiply(s - 1, n)
             if s - 1 == LAST_CHUNK:
                 for n in range(BANKS_PER_CHUNK):
                     quantise(LAST_CHUNK, n * BANK, BANK)

@@ -28,9 +28,9 @@ UNITS = N_OUT // CHUNK
 N_CHUNKS = MODELS * PASSES * UNITS
 LAST_CHUNK = N_CHUNKS - 1
 BANKS_PER_CHUNK = CHUNK // BANK
-BASE_COLS = 448
-COLS_PER_BANK = 80
-HEAD_COLS = (0, 128)
+BASE_COLS = 528
+COLS_PER_BANK = 64
+HEAD_COLS = (256, 512)
 PE_CHUNKS = range(2, 11)
 PE_COLS = 256
 PE_MATMUL_COLS = BANK // PACK
@@ -50,28 +50,26 @@ def tile_twomodelblockrouted_pa_kernel(tc, x, W_qkv, ln1, out):
         quantised = ctx.enter_context(tc.tile_pool(name="quantised", bufs=5))
         results = ctx.enter_context(tc.tile_pool(name="results", bufs=UNITS))
 
-        gains = consts.tile([P, MODELS * PASSES, PACK], BF16)
+        gain_cols = consts.tile([P, MODELS * PASSES, PACK], BF16)
         gain_rows = consts.tile([P, K_PASS], BF16)
         nc.vector.memset(gain_rows[:].bitcast(I32), 0)
         eps = consts.tile([P, 1], F32)
         nc.vector.memset(eps[:], EPS)
-        identity = consts.tile([P, P], F32)
+        identity = consts.tile([P, P], BF16)
         make_identity(nc, identity[:])
-        identity_bf16 = consts.tile([P, P], BF16)
-        nc.vector.tensor_copy(out=identity_bf16[:], in_=identity[:])
+        identity_f32 = consts.tile([P, P], F32)
+        make_identity(nc, identity_f32[:])
         warm = consts.tile([P, 1], F32)
         nc.scalar.activation(out=warm[:], in_=eps[:], func=ACT.Sqrt)
 
+        nc.sync.dma_start(
+            out=gain_rows[0 : MODELS * PASSES, :], in_=ln1.rearrange("g (c k) -> (g c) k", c=PASSES)
+        )
         x_rows = []
         for m in range(ROW_TILES):
             x_m = rows_pool.tile([P, H], BF16, name="x_rows", bufs=ROW_TILES)
             nc.sync.dma_start(out=x_m[:], in_=x[m * P : (m + 1) * P, :])
             x_rows.append(x_m)
-            if m == 0:
-                nc.sync.dma_start(
-                    out=gain_rows[0 : MODELS * PASSES, :],
-                    in_=ln1.rearrange("g (c k) -> (g c) k", c=PASSES),
-                )
         w_raw = {}
         for g, first_unit, units in ((0, 0, 1), (0, 1, 1), (0, 2, 1), (1, 0, 1), (1, 1, 2)):
             for c in range(PASSES):
@@ -88,84 +86,6 @@ def tile_twomodelblockrouted_pa_kernel(tc, x, W_qkv, ln1, out):
                 for u in range(units):
                     w_raw[(g, c, first_unit + u)] = raw[:, :, u * CHUNK : (u + 1) * CHUNK]
 
-        h_grouped = consts.tile([P, ROW_TILES, PASSES, P, PACK], BF16, align_bytes=64)
-        h_codes = consts.tile([P, ROW_TILES, PASSES, P], U32, align_bytes=64)
-        h_scales = consts.tile([P, ROW_TILES, PASSES, P], U8, align_bytes=64)
-        with tc.psum_pool(name="head_psum", bufs=8) as head_psum:
-            gains_t = head_psum.tile([P, PACK, P], BF16, name="x_t")
-            for t in range(PACK):
-                nc.tensor.transpose(gains_t[:, t, :], gain_rows[:, t:K_PASS:PACK], identity_bf16[:])
-            sum_sq = []
-            rms = []
-            x_t = {}
-
-            def sum_squares(m):
-                sum_sq.append(small.tile([P, 1], F32, name="sum_sq"))
-                squares = rows_pool.tile([P, H], BF16, name="squares%d" % (m == 1), bufs=1)
-                if m == 1:
-                    nc.vector.scalar_tensor_tensor(
-                        out=squares[:],
-                        in0=x_rows[m][:],
-                        scalar=1.0,
-                        in1=x_rows[m][:],
-                        op0=ALU.mult,
-                        op1=ALU.mult,
-                        accum_out=sum_sq[m][:],
-                    )
-                else:
-                    nc.scalar.activation(
-                        out=squares[:], in_=x_rows[m][:], func=ACT.Square, accum_out=sum_sq[m][:]
-                    )
-
-            def root(m):
-                rms.append(small.tile([P, 1], F32, name="rms"))
-                nc.scalar.activation(
-                    out=rms[m][:], in_=sum_sq[m][:], func=ACT.Sqrt, scale=1.0 / H, bias=eps[:]
-                )
-
-            def scale_and_transpose(m):
-                rstd = small.tile([P, 1], F32, name="rstd")
-                nc.vector.reciprocal(out=rstd[:], in_=rms[m][:])
-                scaled = rows_pool.tile([P, PASSES, PACK, P], F32, name="scaled")
-                for c in range(PASSES):
-                    nc.vector.tensor_scalar_mul(
-                        out=scaled[:, c],
-                        in0=x_rows[m][:, c * K_PASS : (c + 1) * K_PASS].rearrange("p (q t) -> p t q", t=PACK),
-                        scalar1=rstd[:],
-                    )
-                for c in range(PASSES):
-                    x_t[(m, c)] = head_psum.tile([P, PACK, P], F32, name="x_t")
-                    for t in range(PACK):
-                        nc.tensor.transpose(x_t[(m, c)][:, t, :], scaled[:, c, t, :], identity[:])
-
-            def multiply_by_gains(m):
-                g = 0 if m < FIRST_ROW_TILE[1] else 1
-                for c in range(PASSES):
-                    nc.vector.tensor_tensor(
-                        out=h_grouped[:, m, c],
-                        in0=x_t[(m, c)][:].rearrange("p t r -> p r t"),
-                        in1=gains[:, g * PASSES + c, :].unsqueeze(1).to_broadcast([P, P, PACK]),
-                        op=ALU.mult,
-                    )
-
-            sum_squares(0)
-            sum_squares(1)
-            root(0)
-            nc.vector.tensor_copy(
-                out=gains[:], in_=gains_t[:, :, 0 : MODELS * PASSES].rearrange("p t s -> p s t")
-            )
-            for m in range(ROW_TILES):
-                if m + 2 < ROW_TILES:
-                    sum_squares(m + 2)
-                if m + 1 < ROW_TILES:
-                    root(m + 1)
-                scale_and_transpose(m)
-                if m > 0:
-                    multiply_by_gains(m - 1)
-            multiply_by_gains(ROW_TILES - 1)
-
-        acc_psum = ctx.enter_context(tc.psum_pool(name="acc_psum", bufs=6))
-        turn_psum = ctx.enter_context(tc.psum_pool(name="turn_psum", bufs=2))
         turned = {}
         w_grouped = {}
         w_codes = {}
@@ -190,7 +110,7 @@ def tile_twomodelblockrouted_pa_kernel(tc, x, W_qkv, ln1, out):
                 first = CHUNK - PE_COLS + a
                 nc.tensor.matmul(
                     out=turned[i][:, a : a + PE_MATMUL_COLS, :],
-                    lhsT=identity_bf16[:],
+                    lhsT=identity[:],
                     rhs=w_raw[place(i)][:, :, first : first + PE_MATMUL_COLS].rearrange("p t w -> p w t"),
                     start=True,
                     stop=True,
@@ -262,10 +182,110 @@ def tile_twomodelblockrouted_pa_kernel(tc, x, W_qkv, ln1, out):
                 in_=out_rows[i][:, :, first : first + width],
             )
 
+        h_grouped = consts.tile([P, ROW_TILES, PASSES, P, PACK], BF16, align_bytes=64)
+        h_codes = consts.tile([P, ROW_TILES, PASSES, P], U32, align_bytes=64)
+        h_scales = consts.tile([P, ROW_TILES, PASSES, P], U8, align_bytes=64)
+        with tc.psum_pool(name="head_psum", bufs=1) as head_psum:
+            sum_sq = []
+            rms = []
+            rstd = []
+            h_t = []
+
+            def sum_squares(m):
+                sum_sq.append(small.tile([P, 1], F32, name="sum_sq"))
+                squares = rows_pool.tile([P, H], BF16, name="squares%d" % (m == 1), bufs=1)
+                if m == 1:
+                    nc.vector.scalar_tensor_tensor(
+                        out=squares[:],
+                        in0=x_rows[m][:],
+                        scalar=1.0,
+                        in1=x_rows[m][:],
+                        op0=ALU.mult,
+                        op1=ALU.mult,
+                        accum_out=sum_sq[m][:],
+                    )
+                else:
+                    nc.scalar.activation(
+                        out=squares[:], in_=x_rows[m][:], func=ACT.Square, accum_out=sum_sq[m][:]
+                    )
+
+            def root(m):
+                rms.append(small.tile([P, 1], F32, name="rms"))
+                nc.scalar.activation(
+                    out=rms[m][:], in_=sum_sq[m][:], func=ACT.Sqrt, scale=1.0 / H, bias=eps[:]
+                )
+
+            def invert(m):
+                rstd.append(small.tile([P, 1], F32, name="rstd"))
+                nc.vector.reciprocal(out=rstd[m][:], in_=rms[m][:])
+
+            def normalise(m, h_m, c):
+                nc.vector.scalar_tensor_tensor(
+                    out=h_m[:, c * K_PASS : (c + 1) * K_PASS],
+                    in0=x_rows[m][:, c * K_PASS : (c + 1) * K_PASS],
+                    scalar=rstd[m][:],
+                    in1=gains[0 if m < FIRST_ROW_TILE[1] else 1][:, c * K_PASS : (c + 1) * K_PASS],
+                    op0=ALU.mult,
+                    op1=ALU.mult,
+                )
+
+            def transpose(m, h_m):
+                words = h_m[:].bitcast(F32)
+                h_t.append(head_psum.tile([P, PASSES, P, 2], F32, name="h_t", bufs=ROW_TILES))
+                for c in range(PASSES):
+                    for u in range(2):
+                        nc.tensor.transpose(
+                            h_t[m][:, c, :, u],
+                            words[:, c * K_PASS // 2 + u : (c + 1) * K_PASS // 2 : 2],
+                            identity_f32[:],
+                        )
+
+            gains_t = head_psum.tile([P, PACK, P], BF16, name="gains_t")
+            for b in range(PACK):
+                nc.tensor.transpose(gains_t[:, b, :], gain_rows[:, b * P : (b + 1) * P], identity[:])
+            nc.vector.tensor_copy(
+                out=gain_cols[:], in_=gains_t[:, :, 0 : MODELS * PASSES].rearrange("p b s -> p s b")
+            )
+            gains = []
+            for g in range(MODELS):
+                gains_g = head_psum.tile([P, H], BF16, name="gains", bufs=MODELS)
+                for c in range(PASSES):
+                    for b in range(PACK):
+                        k = c * K_PASS + b * P
+                        nc.tensor.transpose(
+                            gains_g[:, k : k + P],
+                            gain_cols[:, g * PASSES + c, b : b + 1].to_broadcast([P, P]),
+                            identity[:],
+                        )
+                gains.append(gains_g)
+            sum_squares(0)
+            sum_squares(1)
+            root(0)
+            for m in range(2, ROW_TILES):
+                sum_squares(m)
+                root(m - 1)
+            root(ROW_TILES - 1)
+            invert(0)
+            for m in range(ROW_TILES):
+                h_m = rows_pool.tile([P, H], BF16, name="h_rows")
+                normalise(m, h_m, 0)
+                if m + 1 < ROW_TILES:
+                    invert(m + 1)
+                normalise(m, h_m, 1)
+                transpose(m, h_m)
+            regroup(0, HEAD_COLS[0])
+            for m in range(ROW_TILES):
+                nc.scalar.copy(
+                    out=h_grouped[:, m].rearrange("p c r t -> p (c r t)").bitcast(F32),
+                    in_=h_t[m][:].rearrange("p c r u -> p (c r u)"),
+                )
+
+        acc_psum = ctx.enter_context(tc.psum_pool(name="acc_psum", bufs=6))
+        turn_psum = ctx.enter_context(tc.psum_pool(name="turn_psum", bufs=2))
         for s in range(N_CHUNKS + 3):
-            if s < N_CHUNKS:
+            if 0 < s < N_CHUNKS:
                 regroup(s, HEAD_COLS[s] if s < len(HEAD_COLS) else BASE_COLS + COLS_PER_BANK * banks_in_step(s))
-            if s == 1:
+            if s == 2:
                 for m in range(ROW_TILES):
                     nc.vector.quantize_mx(
                         out=h_codes[:, m].rearrange("p c r -> p (c r)").bitcast(FP8X4),

@@ -25,8 +25,14 @@ N_ROW_TILES = (SPLIT // P, (ROWS - SPLIT) // P)
 BANK = 512
 CHUNK = 1024
 UNITS = N_OUT // CHUNK
-N_CHUNKS = MODELS * PASSES * UNITS
+LOADS = tuple((g, c, first, units) for g in range(MODELS) for first, units in ((0, 1), (1, 2)) for c in range(PASSES))
+CHUNKS = [(g, c, first + u) for g, c, first, units in LOADS for u in range(units) if g == 0] + [
+    (1, c, u) for u in range(UNITS) for c in range(PASSES)
+]
+N_CHUNKS = len(CHUNKS)
 LAST_CHUNK = N_CHUNKS - 1
+ACC_BANKS = 6
+EMPTIED_PER_STEP = 3
 BANKS_PER_CHUNK = CHUNK // BANK
 BASE_COLS = 528
 COLS_PER_BANK = 64
@@ -47,7 +53,7 @@ def tile_twomodelblockrouted_pa_kernel(tc, x, W_qkv, ln1, out):
         small = ctx.enter_context(tc.tile_pool(name="small", bufs=ROW_TILES))
         weights = ctx.enter_context(tc.tile_pool(name="weights", bufs=MODELS * PASSES))
         grouped_pool = ctx.enter_context(tc.tile_pool(name="grouped", bufs=3))
-        quantised = ctx.enter_context(tc.tile_pool(name="quantised", bufs=5))
+        quantised = ctx.enter_context(tc.tile_pool(name="quantised", bufs=7))
         results = ctx.enter_context(tc.tile_pool(name="results", bufs=UNITS))
 
         gain_cols = consts.tile([P, MODELS * PASSES, PACK], BF16)
@@ -62,29 +68,28 @@ def tile_twomodelblockrouted_pa_kernel(tc, x, W_qkv, ln1, out):
         warm = consts.tile([P, 1], F32)
         nc.scalar.activation(out=warm[:], in_=eps[:], func=ACT.Sqrt)
 
-        nc.sync.dma_start(
-            out=gain_rows[0 : MODELS * PASSES, :], in_=ln1.rearrange("g (c k) -> (g c) k", c=PASSES)
-        )
         x_rows = []
         for m in range(ROW_TILES):
             x_m = rows_pool.tile([P, H], BF16, name="x_rows", bufs=ROW_TILES)
             nc.sync.dma_start(out=x_m[:], in_=x[m * P : (m + 1) * P, :])
+            if m == 0:
+                nc.sync.dma_start(
+                    out=gain_rows[0 : MODELS * PASSES, :],
+                    in_=ln1.rearrange("g (c k) -> (g c) k", c=PASSES),
+                )
             x_rows.append(x_m)
         w_raw = {}
-        for g, first_unit, units in ((0, 0, 1), (0, 1, 1), (0, 2, 1), (1, 0, 1), (1, 1, 2)):
-            for c in range(PASSES):
-                width = units * CHUNK
-                raw = weights.tile(
-                    [P, PACK, width], BF16, name="w_raw%d" % units, bufs=8 if units == 1 else PASSES
-                )
-                nc.sync.dma_start(
-                    out=raw[:],
-                    in_=W_qkv[
-                        g, c * K_PASS : (c + 1) * K_PASS, first_unit * CHUNK : first_unit * CHUNK + width
-                    ].rearrange("(p t) n -> p t n", t=PACK),
-                )
-                for u in range(units):
-                    w_raw[(g, c, first_unit + u)] = raw[:, :, u * CHUNK : (u + 1) * CHUNK]
+        for g, c, first_unit, units in LOADS:
+            width = units * CHUNK
+            raw = weights.tile([P, PACK, width], BF16, name="w_raw%d" % units)
+            nc.sync.dma_start(
+                out=raw[:],
+                in_=W_qkv[
+                    g, c * K_PASS : (c + 1) * K_PASS, first_unit * CHUNK : first_unit * CHUNK + width
+                ].rearrange("(p t) n -> p t n", t=PACK),
+            )
+            for u in range(units):
+                w_raw[(g, c, first_unit + u)] = raw[:, :, u * CHUNK : (u + 1) * CHUNK]
 
         turned = {}
         w_grouped = {}
@@ -93,16 +98,33 @@ def tile_twomodelblockrouted_pa_kernel(tc, x, W_qkv, ln1, out):
         acc = {}
         out_rows = {}
 
-        def place(i):
-            return i // (PASSES * UNITS), i % PASSES, (i // PASSES) % UNITS
-
-        def bank_group(s):
-            i, n = (s - 2, 0) if s % PASSES == 1 else (s - 3, 1)
-            return (i, n) if 0 < i < N_CHUNKS else None
+        formed = []
+        emptied = []
+        waiting = []
+        filled = []
+        used_banks = 0
+        while len(formed) < N_CHUNKS + 1 or waiting or filled:
+            done = len(formed) - 1
+            if 0 <= done < N_CHUNKS and CHUNKS[done][1] == PASSES - 1:
+                waiting += [(done, n) for n in range(BANKS_PER_CHUNK)]
+            now_formed = []
+            while waiting and used_banks + N_ROW_TILES[CHUNKS[waiting[0][0]][0]] <= ACC_BANKS:
+                used_banks += N_ROW_TILES[CHUNKS[waiting[0][0]][0]]
+                now_formed.append(waiting[0])
+                waiting = waiting[1:]
+            now_emptied = []
+            n_emptied = 0
+            while filled and n_emptied + N_ROW_TILES[CHUNKS[filled[0][0]][0]] <= EMPTIED_PER_STEP:
+                n_emptied += N_ROW_TILES[CHUNKS[filled[0][0]][0]]
+                now_emptied.append(filled[0])
+                filled = filled[1:]
+            used_banks -= n_emptied
+            filled = filled + now_formed
+            formed.append(now_formed)
+            emptied.append(now_emptied)
 
         def banks_in_step(s):
-            group = bank_group(s)
-            return N_ROW_TILES[place(group[0])[0]] if group else 0
+            return sum(N_ROW_TILES[CHUNKS[i][0]] for i, n in emptied[s])
 
         def turn(i):
             turned[i] = turn_psum.tile([P, PE_COLS, PACK], BF16, name="turned")
@@ -111,13 +133,13 @@ def tile_twomodelblockrouted_pa_kernel(tc, x, W_qkv, ln1, out):
                 nc.tensor.matmul(
                     out=turned[i][:, a : a + PE_MATMUL_COLS, :],
                     lhsT=identity[:],
-                    rhs=w_raw[place(i)][:, :, first : first + PE_MATMUL_COLS].rearrange("p t w -> p w t"),
+                    rhs=w_raw[CHUNKS[i]][:, :, first : first + PE_MATMUL_COLS].rearrange("p t w -> p w t"),
                     start=True,
                     stop=True,
                 )
 
         def regroup(i, vector_cols):
-            g, c, u = place(i)
+            g, c, u = CHUNKS[i]
             raw = w_raw[(g, c, u)]
             grouped = grouped_pool.tile([P, CHUNK, PACK], BF16, name="w_grouped", align_bytes=64)
             if vector_cols:
@@ -145,13 +167,13 @@ def tile_twomodelblockrouted_pa_kernel(tc, x, W_qkv, ln1, out):
             )
 
         def multiply(i, n):
-            g = place(i)[0]
+            g, last_pass, u = CHUNKS[i]
             n_cols = slice(n * BANK, (n + 1) * BANK)
             for r in range(N_ROW_TILES[g]):
                 m = FIRST_ROW_TILE[g] + r
                 acc[(i, n, r)] = acc_psum.tile([P, BANK], F32, name="acc")
                 for c in range(PASSES):
-                    chunk = i - (PASSES - 1 - c)
+                    chunk = CHUNKS.index((g, c, u))
                     nc.tensor.matmul_mx(
                         out=acc[(i, n, r)][:],
                         lhsT=h_codes[:, m, c, :].bitcast(FP8X4),
@@ -163,7 +185,7 @@ def tile_twomodelblockrouted_pa_kernel(tc, x, W_qkv, ln1, out):
                     )
 
         def empty(i, n):
-            g = place(i)[0]
+            g = CHUNKS[i][0]
             if n == 0:
                 out_rows[i] = results.tile([P, N_ROW_TILES[g], CHUNK], F32, name="out_rows%d" % g)
             for r in range(N_ROW_TILES[g]):
@@ -172,7 +194,7 @@ def tile_twomodelblockrouted_pa_kernel(tc, x, W_qkv, ln1, out):
                 )
 
         def store(i, first, width):
-            g, c, u = place(i)
+            g, c, u = CHUNKS[i]
             first_row = FIRST_ROW_TILE[g] * P
             nc.sync.dma_start(
                 out=out[
@@ -280,11 +302,10 @@ def tile_twomodelblockrouted_pa_kernel(tc, x, W_qkv, ln1, out):
                     in_=h_t[m][:].rearrange("p c r u -> p (c r u)"),
                 )
 
-        acc_psum = ctx.enter_context(tc.psum_pool(name="acc_psum", bufs=6))
+        acc_psum = ctx.enter_context(tc.psum_pool(name="acc_psum", bufs=ACC_BANKS))
         turn_psum = ctx.enter_context(tc.psum_pool(name="turn_psum", bufs=2))
-        for s in range(N_CHUNKS + 3):
-            if 0 < s < N_CHUNKS:
-                regroup(s, HEAD_COLS[s] if s < len(HEAD_COLS) else BASE_COLS + COLS_PER_BANK * banks_in_step(s))
+        turns = list(PE_CHUNKS)
+        for s in range(len(formed)):
             if s == 2:
                 for m in range(ROW_TILES):
                     nc.vector.quantize_mx(
@@ -292,21 +313,23 @@ def tile_twomodelblockrouted_pa_kernel(tc, x, W_qkv, ln1, out):
                         scales=h_scales[:, m].rearrange("p c r -> p (c r)"),
                         in_=h_grouped[:, m].rearrange("p c r t -> p (c r t)"),
                     )
+            if 0 < s < N_CHUNKS:
+                regroup(s, HEAD_COLS[s] if s < len(HEAD_COLS) else BASE_COLS + COLS_PER_BANK * banks_in_step(s))
             if 0 <= s - 1 < LAST_CHUNK:
                 quantise(s - 1, 0, CHUNK)
-            for n in range(BANKS_PER_CHUNK):
-                if s % PASSES == 0 and s + 1 + n in PE_CHUNKS:
-                    turn(s + 1 + n)
-                if 0 <= s - 1 < LAST_CHUNK and place(s - 1)[1] == PASSES - 1:
-                    multiply(s - 1, n)
-            if s - 1 == LAST_CHUNK:
-                for n in range(BANKS_PER_CHUNK):
+            if turns and turns[0] == s + 1:
+                turn(turns[0])
+                turns = turns[1:]
+            for j, (i, n) in enumerate(formed[s]):
+                if i == LAST_CHUNK:
                     quantise(LAST_CHUNK, n * BANK, BANK)
-                    multiply(LAST_CHUNK, n)
-            group = bank_group(s)
-            if group:
-                empty(group[0], group[1])
-                if group[0] == LAST_CHUNK:
-                    store(group[0], group[1] * BANK, BANK)
-                elif group[1] == BANKS_PER_CHUNK - 1:
-                    store(group[0], 0, CHUNK)
+                multiply(i, n)
+                if j == 0 and turns and turns[0] == s + 2:
+                    turn(turns[0])
+                    turns = turns[1:]
+            for i, n in emptied[s]:
+                empty(i, n)
+                if i == LAST_CHUNK:
+                    store(i, n * BANK, BANK)
+                elif n == BANKS_PER_CHUNK - 1:
+                    store(i, 0, CHUNK)

@@ -25,10 +25,16 @@ N_ROW_TILES = (SPLIT // P, (ROWS - SPLIT) // P)
 BANK = 512
 CHUNK = 1024
 UNITS = N_OUT // CHUNK
-LOADS = tuple((g, c, first, units) for g in range(MODELS) for first, units in ((0, 1), (1, 2)) for c in range(PASSES))
-CHUNKS = [(g, c, first + u) for g, c, first, units in LOADS for u in range(units) if g == 0] + [
-    (1, c, u) for u in range(UNITS) for c in range(PASSES)
-]
+LOADS = (
+    (0, 0, 0, 1),
+    (0, 1, 0, 1),
+    (0, 0, 1, 2),
+    (0, 1, 1, 2),
+    (1, 0, 0, 1),
+    (1, 0, 1, 2),
+    (1, 1, 0, 3),
+)
+CHUNKS = [(g, c, first + u) for g, c, first, units in LOADS for u in range(units)]
 N_CHUNKS = len(CHUNKS)
 LAST_CHUNK = N_CHUNKS - 1
 ACC_BANKS = 6
@@ -37,7 +43,7 @@ BANKS_PER_CHUNK = CHUNK // BANK
 BASE_COLS = 528
 COLS_PER_BANK = 64
 HEAD_COLS = (256, 512)
-PE_CHUNKS = range(2, 11)
+PE_CHUNKS = [i for i in range(2, N_CHUNKS) if i != CHUNKS.index((1, 0, 0))]
 PE_COLS = 256
 PE_MATMUL_COLS = BANK // PACK
 
@@ -51,9 +57,9 @@ def tile_twomodelblockrouted_pa_kernel(tc, x, W_qkv, ln1, out):
         consts = ctx.enter_context(tc.tile_pool(name="consts", bufs=1))
         rows_pool = ctx.enter_context(tc.tile_pool(name="rows", bufs=2))
         small = ctx.enter_context(tc.tile_pool(name="small", bufs=ROW_TILES))
-        weights = ctx.enter_context(tc.tile_pool(name="weights", bufs=MODELS * PASSES))
+        weights = ctx.enter_context(tc.tile_pool(name="weights", bufs=1))
         grouped_pool = ctx.enter_context(tc.tile_pool(name="grouped", bufs=3))
-        quantised = ctx.enter_context(tc.tile_pool(name="quantised", bufs=7))
+        quantised = ctx.enter_context(tc.tile_pool(name="quantised", bufs=8))
         results = ctx.enter_context(tc.tile_pool(name="results", bufs=UNITS))
 
         gain_cols = consts.tile([P, MODELS * PASSES, PACK], BF16)
@@ -81,7 +87,7 @@ def tile_twomodelblockrouted_pa_kernel(tc, x, W_qkv, ln1, out):
         w_raw = {}
         for g, c, first_unit, units in LOADS:
             width = units * CHUNK
-            raw = weights.tile([P, PACK, width], BF16, name="w_raw%d" % units)
+            raw = weights.tile([P, PACK, width], BF16, name="w_raw%d" % units, bufs=sum(load[3] == units for load in LOADS))
             nc.sync.dma_start(
                 out=raw[:],
                 in_=W_qkv[
@@ -304,7 +310,7 @@ def tile_twomodelblockrouted_pa_kernel(tc, x, W_qkv, ln1, out):
 
         acc_psum = ctx.enter_context(tc.psum_pool(name="acc_psum", bufs=ACC_BANKS))
         turn_psum = ctx.enter_context(tc.psum_pool(name="turn_psum", bufs=2))
-        turns = list(PE_CHUNKS)
+        turns = PE_CHUNKS
         for s in range(len(formed)):
             if s == 2:
                 for m in range(ROW_TILES):

@@ -40,7 +40,7 @@ LAST_CHUNK = N_CHUNKS - 1
 ACC_BANKS = 6
 EMPTIED_PER_STEP = 3
 BANKS_PER_CHUNK = CHUNK // BANK
-BASE_COLS = 528
+BASE_COLS = 512
 COLS_PER_BANK = 64
 HEAD_COLS = (256, 512)
 PE_CHUNKS = [i for i in range(2, N_CHUNKS) if i != CHUNKS.index((1, 0, 0))]
@@ -335,7 +335,7 @@ def tile_twomodelblockrouted_pa_kernel(tc, x, W_qkv, ln1, out):
                     turns = turns[1:]
             for i, n in emptied[s]:
                 empty(i, n)
-                if i == LAST_CHUNK:
+                if CHUNKS[i][0] == MODELS - 1:
                     store(i, n * BANK, BANK)
                 elif n == BANKS_PER_CHUNK - 1:
                     store(i, 0, CHUNK)

from contextlib import ExitStack

import concourse.mybir as mybir
from concourse.masks import make_identity

F32 = mybir.dt.float32
BF16 = mybir.dt.bfloat16
I32 = mybir.dt.int32
U32 = mybir.dt.uint32
U8 = mybir.dt.uint8
FP8X4 = mybir.dt.float8_e4m3fn_x4
ALU = mybir.AluOpType
ACT = mybir.ActivationFunctionType

P = 128
PACK = 4
K_PASS = P * PACK
ROWS, SPLIT, H, N_OUT = 512, 384, 1024, 3072
EPS = 1.1920929e-07
MODELS = 2
PASSES = H // K_PASS
ROW_TILES = ROWS // P
FIRST_ROW_TILE = (0, SPLIT // P)
N_ROW_TILES = (SPLIT // P, (ROWS - SPLIT) // P)
BANK = 512
CHUNK = 1024
UNITS = N_OUT // CHUNK
LOADS = (
    (0, 0, 0, 1),
    (0, 1, 0, 1),
    (0, 0, 1, 2),
    (0, 1, 1, 2),
    (1, 0, 0, 1),
    (1, 0, 1, 2),
    (1, 1, 0, 3),
)
CHUNKS = [(g, c, first + u) for g, c, first, units in LOADS for u in range(units)]
N_CHUNKS = len(CHUNKS)
LAST_CHUNK = N_CHUNKS - 1
ACC_BANKS = 6
EMPTIED_PER_STEP = 3
BANKS_PER_CHUNK = CHUNK // BANK
BASE_COLS = 512
COLS_PER_BANK = 64
HEAD_COLS = (256, 512)
PE_CHUNKS = [i for i in range(2, N_CHUNKS) if i != CHUNKS.index((1, 0, 0))]
PE_COLS = 256
PE_MATMUL_COLS = BANK // PACK

FLOPS = 2 * ROWS * H * N_OUT


def tile_twomodelblockrouted_pa_kernel(tc, x, W_qkv, ln1, out):
    nc = tc.nc
    with ExitStack() as ctx:
        ctx.enter_context(tc.manual_schedule())
        consts = ctx.enter_context(tc.tile_pool(name="consts", bufs=1))
        rows_pool = ctx.enter_context(tc.tile_pool(name="rows", bufs=2))
        small = ctx.enter_context(tc.tile_pool(name="small", bufs=ROW_TILES))
        weights = ctx.enter_context(tc.tile_pool(name="weights", bufs=1))
        grouped_pool = ctx.enter_context(tc.tile_pool(name="grouped", bufs=3))
        quantised = ctx.enter_context(tc.tile_pool(name="quantised", bufs=8))
        results = ctx.enter_context(tc.tile_pool(name="results", bufs=UNITS))

        gain_cols = consts.tile([P, MODELS * PASSES, PACK], BF16)
        gain_rows = consts.tile([P, K_PASS], BF16)
        nc.vector.memset(gain_rows[:].bitcast(I32), 0)
        eps = consts.tile([P, 1], F32)
        nc.vector.memset(eps[:], EPS)
        identity = consts.tile([P, P], BF16)
        make_identity(nc, identity[:])
        identity_f32 = consts.tile([P, P], F32)
        make_identity(nc, identity_f32[:])
        warm = consts.tile([P, 1], F32)
        nc.scalar.activation(out=warm[:], in_=eps[:], func=ACT.Sqrt)

        x_rows = []
        for m in range(ROW_TILES):
            x_m = rows_pool.tile([P, H], BF16, name="x_rows", bufs=ROW_TILES)
            nc.sync.dma_start(out=x_m[:], in_=x[m * P : (m + 1) * P, :])
            if m == 0:
                nc.sync.dma_start(
                    out=gain_rows[0 : MODELS * PASSES, :],
                    in_=ln1.rearrange("g (c k) -> (g c) k", c=PASSES),
                )
            x_rows.append(x_m)
        w_raw = {}
        for g, c, first_unit, units in LOADS:
            width = units * CHUNK
            raw = weights.tile([P, PACK, width], BF16, name="w_raw%d" % units, bufs=sum(load[3] == units for load in LOADS))
            nc.sync.dma_start(
                out=raw[:],
                in_=W_qkv[
                    g, c * K_PASS : (c + 1) * K_PASS, first_unit * CHUNK : first_unit * CHUNK + width
                ].rearrange("(p t) n -> p t n", t=PACK),
            )
            for u in range(units):
                w_raw[(g, c, first_unit + u)] = raw[:, :, u * CHUNK : (u + 1) * CHUNK]

        turned = {}
        w_grouped = {}
        w_codes = {}
        w_scales = {}
        acc = {}
        out_rows = {}

        formed = []
        emptied = []
        waiting = []
        filled = []
        used_banks = 0
        while len(formed) < N_CHUNKS + 1 or waiting or filled:
            done = len(formed) - 1
            if 0 <= done < N_CHUNKS and CHUNKS[done][1] == PASSES - 1:
                waiting += [(done, n) for n in range(BANKS_PER_CHUNK)]
            now_formed = []
            while waiting and used_banks + N_ROW_TILES[CHUNKS[waiting[0][0]][0]] <= ACC_BANKS:
                used_banks += N_ROW_TILES[CHUNKS[waiting[0][0]][0]]
                now_formed.append(waiting[0])
                waiting = waiting[1:]
            now_emptied = []
            n_emptied = 0
            while filled and n_emptied + N_ROW_TILES[CHUNKS[filled[0][0]][0]] <= EMPTIED_PER_STEP:
                n_emptied += N_ROW_TILES[CHUNKS[filled[0][0]][0]]
                now_emptied.append(filled[0])
                filled = filled[1:]
            used_banks -= n_emptied
            filled = filled + now_formed
            formed.append(now_formed)
            emptied.append(now_emptied)

        def banks_in_step(s):
            return sum(N_ROW_TILES[CHUNKS[i][0]] for i, n in emptied[s])

        def turn(i):
            turned[i] = turn_psum.tile([P, PE_COLS, PACK], BF16, name="turned")
            for a in range(0, PE_COLS, PE_MATMUL_COLS):
                first = CHUNK - PE_COLS + a
                nc.tensor.matmul(
                    out=turned[i][:, a : a + PE_MATMUL_COLS, :],
                    lhsT=identity[:],
                    rhs=w_raw[CHUNKS[i]][:, :, first : first + PE_MATMUL_COLS].rearrange("p t w -> p w t"),
                    start=True,
                    stop=True,
                )

        def regroup(i, vector_cols):
            g, c, u = CHUNKS[i]
            raw = w_raw[(g, c, u)]
            grouped = grouped_pool.tile([P, CHUNK, PACK], BF16, name="w_grouped", align_bytes=64)
            if vector_cols:
                nc.vector.tensor_copy(
                    out=grouped[:, 0:vector_cols, :].rearrange("p (w i) t -> p w t i", i=4),
                    in_=raw[:, :, 0:vector_cols].rearrange("p t (w i) -> p w t i", i=4),
                )
            direct_end = CHUNK - PE_COLS if i in PE_CHUNKS else CHUNK
            nc.scalar.copy(
                out=grouped[:, vector_cols:direct_end, :].rearrange("p (w i) t -> p w t i", i=4),
                in_=raw[:, :, vector_cols:direct_end].rearrange("p t (w i) -> p w t i", i=4),
            )
            if i in PE_CHUNKS:
                nc.scalar.copy(out=grouped[:, direct_end:CHUNK, :], in_=turned[i][:])
            w_grouped[i] = grouped

        def quantise(i, first, width):
            if first == 0:
                w_codes[i] = quantised.tile([P, CHUNK], U32, name="w_codes", align_bytes=64)
                w_scales[i] = quantised.tile([P, CHUNK], U8, name="w_scales", align_bytes=64)
            nc.vector.quantize_mx(
                out=w_codes[i][:, first : first + width].bitcast(FP8X4),
                scales=w_scales[i][:, first : first + width],
                in_=w_grouped[i][:, first : first + width, :].rearrange("p w t -> p (w t)"),
            )

        def multiply(i, n):
            g, last_pass, u = CHUNKS[i]
            n_cols = slice(n * BANK, (n + 1) * BANK)
            for r in range(N_ROW_TILES[g]):
                m = FIRST_ROW_TILE[g] + r
                acc[(i, n, r)] = acc_psum.tile([P, BANK], F32, name="acc")
                for c in range(PASSES):
                    chunk = CHUNKS.index((g, c, u))
                    nc.tensor.matmul_mx(
                        out=acc[(i, n, r)][:],
                        lhsT=h_codes[:, m, c, :].bitcast(FP8X4),
                        lhsT_scale=h_scales[:, m, c, :],
                        rhs=w_codes[chunk][:, n_cols].bitcast(FP8X4),
                        rhs_scale=w_scales[chunk][:, n_cols],
                        start=(c == 0),
                        stop=(c == PASSES - 1),
                    )

        def empty(i, n):
            g = CHUNKS[i][0]
            if n == 0:
                out_rows[i] = results.tile([P, N_ROW_TILES[g], CHUNK], F32, name="out_rows%d" % g)
            for r in range(N_ROW_TILES[g]):
                nc.scalar.copy(
                    out=out_rows[i][:, r, n * BANK : (n + 1) * BANK], in_=acc[(i, n, r)][:]
                )

        def store(i, first, width):
            g, c, u = CHUNKS[i]
            first_row = FIRST_ROW_TILE[g] * P
            nc.sync.dma_start(
                out=out[
                    first_row : first_row + N_ROW_TILES[g] * P,
                    u * CHUNK + first : u * CHUNK + first + width,
                ].rearrange("(r p) n -> p r n", p=P),
                in_=out_rows[i][:, :, first : first + width],
            )

        h_grouped = consts.tile([P, ROW_TILES, PASSES, P, PACK], BF16, align_bytes=64)
        h_codes = consts.tile([P, ROW_TILES, PASSES, P], U32, align_bytes=64)
        h_scales = consts.tile([P, ROW_TILES, PASSES, P], U8, align_bytes=64)
        with tc.psum_pool(name="head_psum", bufs=1) as head_psum:
            sum_sq = []
            rms = []
            rstd = []
            h_t = []

            def sum_squares(m):
                sum_sq.append(small.tile([P, 1], F32, name="sum_sq"))
                squares = rows_pool.tile([P, H], BF16, name="squares%d" % (m == 1), bufs=1)
                if m == 1:
                    nc.vector.scalar_tensor_tensor(
                        out=squares[:],
                        in0=x_rows[m][:],
                        scalar=1.0,
                        in1=x_rows[m][:],
                        op0=ALU.mult,
                        op1=ALU.mult,
                        accum_out=sum_sq[m][:],
                    )
                else:
                    nc.scalar.activation(
                        out=squares[:], in_=x_rows[m][:], func=ACT.Square, accum_out=sum_sq[m][:]
                    )

            def root(m):
                rms.append(small.tile([P, 1], F32, name="rms"))
                nc.scalar.activation(
                    out=rms[m][:], in_=sum_sq[m][:], func=ACT.Sqrt, scale=1.0 / H, bias=eps[:]
                )

            def invert(m):
                rstd.append(small.tile([P, 1], F32, name="rstd"))
                nc.vector.reciprocal(out=rstd[m][:], in_=rms[m][:])

            def normalise(m, h_m, c):
                nc.vector.scalar_tensor_tensor(
                    out=h_m[:, c * K_PASS : (c + 1) * K_PASS],
                    in0=x_rows[m][:, c * K_PASS : (c + 1) * K_PASS],
                    scalar=rstd[m][:],
                    in1=gains[0 if m < FIRST_ROW_TILE[1] else 1][:, c * K_PASS : (c + 1) * K_PASS],
                    op0=ALU.mult,
                    op1=ALU.mult,
                )

            def transpose(m, h_m):
                words = h_m[:].bitcast(F32)
                h_t.append(head_psum.tile([P, PASSES, P, 2], F32, name="h_t", bufs=ROW_TILES))
                for c in range(PASSES):
                    for u in range(2):
                        nc.tensor.transpose(
                            h_t[m][:, c, :, u],
                            words[:, c * K_PASS // 2 + u : (c + 1) * K_PASS // 2 : 2],
                            identity_f32[:],
                        )

            gains_t = head_psum.tile([P, PACK, P], BF16, name="gains_t")
            for b in range(PACK):
                nc.tensor.transpose(gains_t[:, b, :], gain_rows[:, b * P : (b + 1) * P], identity[:])
            nc.vector.tensor_copy(
                out=gain_cols[:], in_=gains_t[:, :, 0 : MODELS * PASSES].rearrange("p b s -> p s b")
            )
            gains = []
            for g in range(MODELS):
                gains_g = head_psum.tile([P, H], BF16, name="gains", bufs=MODELS)
                for c in range(PASSES):
                    for b in range(PACK):
                        k = c * K_PASS + b * P
                        nc.tensor.transpose(
                            gains_g[:, k : k + P],
                            gain_cols[:, g * PASSES + c, b : b + 1].to_broadcast([P, P]),
                            identity[:],
                        )
                gains.append(gains_g)
            sum_squares(0)
            sum_squares(1)
            root(0)
            for m in range(2, ROW_TILES):
                sum_squares(m)
                root(m - 1)
            root(ROW_TILES - 1)
            invert(0)
            for m in range(ROW_TILES):
                h_m = rows_pool.tile([P, H], BF16, name="h_rows")
                normalise(m, h_m, 0)
                if m + 1 < ROW_TILES:
                    invert(m + 1)
                normalise(m, h_m, 1)
                transpose(m, h_m)
            regroup(0, HEAD_COLS[0])
            for m in range(ROW_TILES):
                nc.scalar.copy(
                    out=h_grouped[:, m].rearrange("p c r t -> p (c r t)").bitcast(F32),
                    in_=h_t[m][:].rearrange("p c r u -> p (c r u)"),
                )

        acc_psum = ctx.enter_context(tc.psum_pool(name="acc_psum", bufs=ACC_BANKS))
        turn_psum = ctx.enter_context(tc.psum_pool(name="turn_psum", bufs=2))
        turns = PE_CHUNKS
        for s in range(len(formed)):
            if s == 2:
                for m in range(ROW_TILES):
                    nc.vector.quantize_mx(
                        out=h_codes[:, m].rearrange("p c r -> p (c r)").bitcast(FP8X4),
                        scales=h_scales[:, m].rearrange("p c r -> p (c r)"),
                        in_=h_grouped[:, m].rearrange("p c r t -> p (c r t)"),
                    )
            if 0 < s < N_CHUNKS:
                regroup(s, HEAD_COLS[s] if s < len(HEAD_COLS) else BASE_COLS + COLS_PER_BANK * banks_in_step(s))
            if 0 <= s - 1 < LAST_CHUNK:
                quantise(s - 1, 0, CHUNK)
            if turns and turns[0] == s + 1:
                turn(turns[0])
                turns = turns[1:]
            for j, (i, n) in enumerate(formed[s]):
                if i == LAST_CHUNK:
                    quantise(LAST_CHUNK, n * BANK, BANK)
                multiply(i, n)
                if j == 0 and turns and turns[0] == s + 2:
                    turn(turns[0])
                    turns = turns[1:]
            for i, n in emptied[s]:
                empty(i, n)
                if CHUNKS[i][0] == MODELS - 1:
                    store(i, n * BANK, BANK)
                elif n == BANKS_PER_CHUNK - 1:
                    store(i, 0, CHUNK)
